import numpy as np
import ml_dtypes


def mxq(x, axis, fmt="e4m3"):
    dtype, down = {"e4m3": (ml_dtypes.float8_e4m3fn, 7), "e5m2": (ml_dtypes.float8_e5m2, 14)}[fmt]
    v = np.moveaxis(np.asarray(x, np.float32).astype(ml_dtypes.bfloat16).astype(np.float64), axis, -1)
    blocks = v.reshape(v.shape[:-1] + (-1, 32))
    amax = np.abs(blocks).max(-1, keepdims=True)
    byte = np.maximum(np.where(amax > 0, np.frexp(amax)[1] - 1 + 127, 0) - down, 1)
    scale = np.exp2(byte - 127.0)
    codes = (blocks / scale).astype(np.float32).astype(dtype).astype(np.float64)
    return np.moveaxis((codes * scale).reshape(v.shape), -1, axis)


WIDE = False


def mx_kscale(k):
    if not WIDE:
        return np.ones(k)
    levels = np.array([10, -10, 5, -5, 0])
    a = np.random.permutation(np.resize(levels, k // 512 * 4)).reshape(k // 512, 4)
    idx = np.arange(k)
    return np.exp2(a[idx // 512, idx % 128 // 32])


BF16 = ml_dtypes.bfloat16


def bf(x):
    return np.asarray(x, np.float32).astype(BF16)


def f64(x):
    return np.asarray(x).astype(np.float64)


B, D, MP, MID, L = 1024, 768, 1024, 1024, 4
HALF = D // 2


def setup_inputs():
    s = mx_kscale(MP)
    t = mx_kscale(MID)
    return {
        "x": bf(np.random.standard_normal((B, D))),
        "h_prev": bf(np.maximum(np.random.standard_normal((B, MP)) * np.sqrt(2.0), 0.0) * s),
        "w_hid": bf(np.random.standard_normal((MP, MID)) * np.sqrt(2.0 / MP) / s[:, None] * t),
        "b_hid": bf(np.random.standard_normal(MID) * 0.2 * t),
        "w_out": bf(np.random.standard_normal((MID, HALF)) / np.sqrt(MID) / t[:, None]),
        "b_out": bf(np.random.standard_normal(HALF) * 0.2),
    }


def reference(x, h_prev, w_hid, b_hid, w_out, b_out):
    x = f64(x)
    first = x[:, 0::2]
    second = x[:, 1::2]
    h = np.maximum((mxq(f64(h_prev), 1, "e4m3") @ mxq(f64(w_hid), 0, "e4m3")) + f64(b_hid), 0.0)
    shift = (mxq(h, 1, "e4m3") @ mxq(f64(w_out), 0, "e4m3")) + f64(b_out)
    y_second = second + shift
    return np.stack([first, y_second], axis=2).reshape(x.shape)

@@ -1,0 +1,279 @@
+from contextlib import ExitStack
+
+import concourse.mybir as mybir
+from concourse.masks import make_identity
+
+F32 = mybir.dt.float32
+BF16 = mybir.dt.bfloat16
+U32 = mybir.dt.uint32
+U8 = mybir.dt.uint8
+FP8X4 = mybir.dt.float8_e4m3fn_x4
+ADD = mybir.AluOpType.add
+RELU = mybir.ActivationFunctionType.Relu
+IDENTITY = mybir.ActivationFunctionType.Identity
+
+P = 128
+PACK = 4
+K_PASS = P * PACK
+B, D, MP, MID = 1024, 768, 1024, 1024
+HALF = D // 2
+B_TILES = B // P
+B_HALF = 512
+PASSES = MP // K_PASS
+MID_TILES = MID // P
+J_TILES = HALF // P
+
+FLOPS = 2 * B * MP * MID + 2 * B * MID * HALF
+
+
+def tile_additivecoupling_pa_kernel(tc, x, h_prev, w_hid, b_hid, w_out, b_out, out):
+    nc = tc.nc
+    with ExitStack() as ctx:
+        keep = ctx.enter_context(tc.tile_pool(name="keep", bufs=1))
+        y_pool = ctx.enter_context(tc.tile_pool(name="y_pool", bufs=4))
+        psum_acc = ctx.enter_context(tc.psum_pool(name="psum_acc", bufs=4))
+        psum_t = ctx.enter_context(tc.psum_pool(name="psum_t", bufs=2))
+        psum_y = ctx.enter_context(tc.psum_pool(name="psum_y", bufs=1))
+
+        hp_rows = keep.tile([P, B_TILES, MP], BF16)
+        hp_grouped = keep.tile([P, PASSES, B * PACK], BF16, align_bytes=64)
+        hp_codes = keep.tile([P, PASSES, B], U32, align_bytes=64)
+        hp_scales = keep.tile([P, PASSES, B], U8, align_bytes=64)
+
+        w_raw = keep.tile([P, 2, PASSES, PACK, 512], BF16)
+        w_grouped = keep.tile([P, 2, PASSES, 512 * PACK], BF16, align_bytes=64)
+        w_codes = keep.tile([P, PASSES, MID], U32, align_bytes=64)
+        w_scales = keep.tile([P, PASSES, MID], U8, align_bytes=64)
+
+        h_rows = keep.tile([P, PASSES, PACK, B], BF16)
+        h_grouped = keep.tile([P, PASSES, B * PACK], BF16, align_bytes=64)
+        h_codes = keep.tile([P, PASSES, B], U32, align_bytes=64)
+        h_scales = keep.tile([P, PASSES, B], U8, align_bytes=64)
+
+        wo_raw = keep.tile([P, PASSES, PACK, HALF], BF16)
+        wo_grouped = keep.tile([P, PASSES * HALF * PACK], BF16, align_bytes=64)
+        wo_codes = keep.tile([P, PASSES * HALF], U32, align_bytes=64)
+        wo_scales = keep.tile([P, PASSES * HALF], U8, align_bytes=64)
+
+        x_rows = keep.tile([P, B_TILES, D], BF16)
+        shift_t = keep.tile([P, J_TILES, B], F32)
+
+        ident_f32 = keep.tile([P, P], F32)
+        ident_bf16 = keep.tile([P, P], BF16)
+        zeros_f32 = keep.tile([P, P], F32)
+        bias_rows = keep.tile([P, P], BF16)
+        bias_col = keep.tile([P, MID_TILES + J_TILES], F32)
+
+        y_banks = [psum_y.tile([P, 1 + J_TILES, P], F32, name="y_bank%d" % i) for i in range(2)]
+
+        nc.vector.memset(bias_rows[:], 0.0)
+        nc.vector.memset(zeros_f32[:], 0.0)
+        nc.scalar.dma_start(out=bias_rows[0:MID_TILES, :], in_=b_hid.rearrange("(m p) -> m p", p=P))
+        nc.scalar.dma_start(
+            out=bias_rows[MID_TILES : MID_TILES + J_TILES, :], in_=b_out.rearrange("(m p) -> m p", p=P)
+        )
+
+        def load_h_prev(bt):
+            nc.sync.dma_start(out=hp_rows[:, bt, :], in_=h_prev[bt * P : (bt + 1) * P, :])
+
+        def load_w_hid(mh):
+            for g in range(PASSES):
+                for u in range(2):
+                    r0 = K_PASS * g + 256 * u
+                    nc.sync.dma_start(
+                        out=w_raw[:, mh, g, 2 * u : 2 * u + 2, :],
+                        in_=w_hid[r0 : r0 + 256, 512 * mh : 512 * mh + 512].rearrange("(q e) c -> q e c", e=2),
+                    )
+
+        load_w_hid(0)
+        for bt in range(4):
+            load_h_prev(bt)
+        nc.sync.dma_start(
+            out=wo_raw[:].rearrange("p g t n -> p (g t) n"),
+            in_=w_out.rearrange("(s p) n -> p s n", p=P),
+        )
+        for bt in range(4, 8):
+            load_h_prev(bt)
+        load_w_hid(1)
+        for xh in range(2):
+            nc.sync.dma_start(
+                out=x_rows[:, 4 * xh : 4 * xh + 4, :],
+                in_=x[B_HALF * xh : B_HALF * (xh + 1), :].rearrange("(t p) d -> p t d", p=P),
+            )
+
+        make_identity(nc, ident_f32[:])
+        nc.vector.tensor_copy(out=ident_bf16[:], in_=ident_f32[:])
+
+        def spread_biases():
+            bias_t = psum_t.tile([P, P], BF16, tag="bank")
+            nc.tensor.transpose(bias_t[:], bias_rows[:], ident_bf16[:])
+            nc.vector.tensor_copy(out=bias_col[:], in_=bias_t[:, 0 : MID_TILES + J_TILES])
+            for bank in y_banks:
+                nc.tensor.transpose(bank[:, 0, :], zeros_f32[:], ident_f32[:])
+
+        def transpose_h_prev(bt):
+            words = hp_rows[:, bt, :].bitcast(F32)
+            pairs_t = psum_t.tile([P, 2 * PASSES, P], F32, tag="bank")
+            for s in range(2 * PASSES):
+                nc.tensor.transpose(pairs_t[:, s, :], words[:, s * P : (s + 1) * P], ident_f32[:])
+            nc.scalar.copy(
+                out=hp_grouped[:, :, bt * P * PACK : (bt + 1) * P * PACK]
+                .bitcast(F32)
+                .rearrange("q g (b u) -> q g b u", u=2),
+                in_=pairs_t[:].rearrange("q (g u) b -> q g b u", u=2),
+            )
+
+        def quantise_h_prev(pair):
+            cols = slice(pair * 2 * P, (pair + 1) * 2 * P)
+            wide = slice(pair * 2 * P * PACK, (pair + 1) * 2 * P * PACK)
+            for g in range(PASSES):
+                nc.vector.quantize_mx(
+                    out=hp_codes[:, g, cols].bitcast(FP8X4), scales=hp_scales[:, g, cols], in_=hp_grouped[:, g, wide]
+                )
+
+        def regroup(dst, src):
+            nc.vector.tensor_copy(
+                out=dst.rearrange("p (c i) t -> p c t i", i=4),
+                in_=src.rearrange("p t (c i) -> p c t i", i=4),
+            )
+
+        def regroup_w_hid(mh):
+            for g in range(PASSES):
+                dst = w_grouped[:, mh, g, :].rearrange("p (c t) -> p c t", t=PACK)
+                src = w_raw[:, mh, g, :, :]
+                regroup(dst, src)
+
+        def quantise_w_hid(mh):
+            for g in range(PASSES):
+                nc.vector.quantize_mx(
+                    out=w_codes[:, g, 512 * mh : 512 * mh + 512].bitcast(FP8X4),
+                    scales=w_scales[:, g, 512 * mh : 512 * mh + 512],
+                    in_=w_grouped[:, mh, g, :],
+                )
+
+        def hidden_matmuls(mh, bh):
+            cols = slice(bh * B_HALF, (bh + 1) * B_HALF)
+            for t in range(PACK):
+                mt = PACK * mh + t
+                acc = psum_acc.tile([P, B_HALF], F32, tag="acc")
+                for g in range(PASSES):
+                    nc.tensor.matmul_mx(
+                        out=acc[:],
+                        lhsT=w_codes[:, g, mt * P : (mt + 1) * P].bitcast(FP8X4),
+                        lhsT_scale=w_scales[:, g, mt * P : (mt + 1) * P],
+                        rhs=hp_codes[:, g, cols].bitcast(FP8X4),
+                        rhs_scale=hp_scales[:, g, cols],
+                        start=(g == 0),
+                        stop=(g == PASSES - 1),
+                    )
+                nc.scalar.activation(
+                    out=h_rows[:, mh, t, cols], in_=acc[:], func=RELU, bias=bias_col[:, mt : mt + 1], scale=1.0
+                )
+
+        def quantise_hidden(mh, bh):
+            cols = slice(bh * B_HALF, (bh + 1) * B_HALF)
+            wide = slice(bh * B_HALF * PACK, (bh + 1) * B_HALF * PACK)
+            regroup(
+                h_grouped[:, mh, wide].rearrange("p (c t) -> p c t", t=PACK),
+                h_rows[:, mh, :, cols],
+            )
+            nc.vector.quantize_mx(
+                out=h_codes[:, mh, cols].bitcast(FP8X4), scales=h_scales[:, mh, cols], in_=h_grouped[:, mh, wide]
+            )
+
+        def regroup_w_out():
+            for g in range(PASSES):
+                regroup(
+                    wo_grouped[:, g * HALF * PACK : (g + 1) * HALF * PACK].rearrange("p (c t) -> p c t", t=PACK),
+                    wo_raw[:, g, :, :],
+                )
+
+        def quantise_w_out():
+            for c0, c1 in ((0, 512), (512, PASSES * HALF)):
+                nc.vector.quantize_mx(
+                    out=wo_codes[:, c0:c1].bitcast(FP8X4),
+                    scales=wo_scales[:, c0:c1],
+                    in_=wo_grouped[:, c0 * PACK : c1 * PACK],
+                )
+
+        def shift_pass(acc, jt, bh, g):
+            cols = slice(bh * B_HALF, (bh + 1) * B_HALF)
+            w0 = g * HALF + jt * P
+            nc.tensor.matmul_mx(
+                out=acc[:],
+                lhsT=wo_codes[:, w0 : w0 + P].bitcast(FP8X4),
+                lhsT_scale=wo_scales[:, w0 : w0 + P],
+                rhs=h_codes[:, g, cols].bitcast(FP8X4),
+                rhs_scale=h_scales[:, g, cols],
+                start=(g == 0),
+                stop=(g == PASSES - 1),
+            )
+
+        def open_shift(bh):
+            accs = [psum_acc.tile([P, B_HALF], F32, tag="acc", name="shift_acc%d" % jt) for jt in range(J_TILES)]
+            for jt in range(J_TILES):
+                shift_pass(accs[jt], jt, bh, 0)
+            return accs
+
+        def close_shift(accs, bh):
+            cols = slice(bh * B_HALF, (bh + 1) * B_HALF)
+            for jt in range(J_TILES):
+                acc = accs[jt]
+                shift_pass(acc, jt, bh, 1)
+                nc.scalar.activation(
+                    out=shift_t[:, jt, cols],
+                    in_=acc[:],
+                    func=IDENTITY,
+                    bias=bias_col[:, MID_TILES + jt : MID_TILES + jt + 1],
+                    scale=1.0,
+                )
+
+        def couple(bt):
+            rows = slice(bt * P, (bt + 1) * P)
+            bank = y_banks[bt % 2]
+            for jt in range(J_TILES):
+                nc.tensor.transpose(bank[:, 1 + jt, :], shift_t[:, jt, rows], ident_f32[:])
+            y = y_pool.tile([P, D], F32)
+            for jt in range(J_TILES):
+                nc.vector.tensor_tensor(
+                    out=y[:, 2 * P * jt : 2 * P * (jt + 1)].rearrange("p (j e) -> p j e", e=2),
+                    in0=bank[:, 0 : 2 + jt : 1 + jt, :].rearrange("p e j -> p j e"),
+                    in1=x_rows[:, bt, 2 * P * jt : 2 * P * (jt + 1)].rearrange("p (j e) -> p j e", e=2),
+                    op=ADD,
+                )
+            nc.sync.dma_start(out=out[rows, :], in_=y[:])
+
+        with tc.manual_schedule():
+            regroup_w_hid(0)
+            transpose_h_prev(0)
+            transpose_h_prev(1)
+            quantise_w_hid(0)
+            quantise_h_prev(0)
+            transpose_h_prev(2)
+            transpose_h_prev(3)
+            spread_biases()
+            quantise_h_prev(1)
+            regroup_w_out()
+            for bt in range(4, 8):
+                transpose_h_prev(bt)
+            hidden_matmuls(0, 0)
+            quantise_w_out()
+            quantise_h_prev(2)
+            quantise_h_prev(3)
+            regroup_w_hid(1)
+            quantise_w_hid(1)
+            hidden_matmuls(0, 1)
+            quantise_hidden(0, 0)
+            hidden_matmuls(1, 0)
+            quantise_hidden(0, 1)
+            hidden_matmuls(1, 1)
+            quantise_hidden(1, 0)
+            shift_0 = open_shift(0)
+            close_shift(shift_0, 0)
+            shift_1 = open_shift(1)
+            quantise_hidden(1, 1)
+            couple(0)
+            couple(1)
+            close_shift(shift_1, 1)
+            for bt in range(2, 8):
+                couple(bt)

@@ -22,6 +22,8 @@ B_HALF = 512
 PASSES = MP // K_PASS
 MID_TILES = MID // P
 J_TILES = HALF // P
+Y_BANKS = 4
+W_PIECE = 256
 
 FLOPS = 2 * B * MP * MID + 2 * B * MID * HALF
 
@@ -30,9 +32,8 @@ def tile_additivecoupling_pa_kernel(tc, x, h_prev, w_hid, b_hid, w_out, b_out, o
     nc = tc.nc
     with ExitStack() as ctx:
         keep = ctx.enter_context(tc.tile_pool(name="keep", bufs=1))
-        y_pool = ctx.enter_context(tc.tile_pool(name="y_pool", bufs=4))
+        y_pool = ctx.enter_context(tc.tile_pool(name="y_pool", bufs=12))
         psum_acc = ctx.enter_context(tc.psum_pool(name="psum_acc", bufs=4))
-        psum_t = ctx.enter_context(tc.psum_pool(name="psum_t", bufs=2))
         psum_y = ctx.enter_context(tc.psum_pool(name="psum_y", bufs=1))
 
         hp_rows = keep.tile([P, B_TILES, MP], BF16)
@@ -64,7 +65,7 @@ def tile_additivecoupling_pa_kernel(tc, x, h_prev, w_hid, b_hid, w_out, b_out, o
         bias_rows = keep.tile([P, P], BF16)
         bias_col = keep.tile([P, MID_TILES + J_TILES], F32)
 
-        y_banks = [psum_y.tile([P, 1 + J_TILES, P], F32, name="y_bank%d" % i) for i in range(2)]
+        y_banks = [psum_y.tile([P, 4, P], F32, name="y_bank%d" % i) for i in range(Y_BANKS)]
 
         nc.vector.memset(bias_rows[:], 0.0)
         nc.vector.memset(zeros_f32[:], 0.0)
@@ -105,15 +106,16 @@ def tile_additivecoupling_pa_kernel(tc, x, h_prev, w_hid, b_hid, w_out, b_out, o
         nc.vector.tensor_copy(out=ident_bf16[:], in_=ident_f32[:])
 
         def spread_biases():
-            bias_t = psum_t.tile([P, P], BF16, tag="bank")
+            bias_t = psum_acc.tile([P, P], BF16, tag="acc")
             nc.tensor.transpose(bias_t[:], bias_rows[:], ident_bf16[:])
             nc.vector.tensor_copy(out=bias_col[:], in_=bias_t[:, 0 : MID_TILES + J_TILES])
             for bank in y_banks:
-                nc.tensor.transpose(bank[:, 0, :], zeros_f32[:], ident_f32[:])
+                for k in range(2):
+                    nc.tensor.transpose(bank[:, 2 * k, :], zeros_f32[:], ident_f32[:])
 
         def transpose_h_prev(bt):
             words = hp_rows[:, bt, :].bitcast(F32)
-            pairs_t = psum_t.tile([P, 2 * PASSES, P], F32, tag="bank")
+            pairs_t = psum_acc.tile([P, 2 * PASSES, P], F32, tag="acc")
             for s in range(2 * PASSES):
                 nc.tensor.transpose(pairs_t[:, s, :], words[:, s * P : (s + 1) * P], ident_f32[:])
             nc.scalar.copy(
@@ -137,19 +139,20 @@ def tile_additivecoupling_pa_kernel(tc, x, h_prev, w_hid, b_hid, w_out, b_out, o
                 in_=src.rearrange("p t (c i) -> p c t i", i=4),
             )
 
-        def regroup_w_hid(mh):
-            for g in range(PASSES):
-                dst = w_grouped[:, mh, g, :].rearrange("p (c t) -> p c t", t=PACK)
-                src = w_raw[:, mh, g, :, :]
-                regroup(dst, src)
-
-        def quantise_w_hid(mh):
-            for g in range(PASSES):
-                nc.vector.quantize_mx(
-                    out=w_codes[:, g, 512 * mh : 512 * mh + 512].bitcast(FP8X4),
-                    scales=w_scales[:, g, 512 * mh : 512 * mh + 512],
-                    in_=w_grouped[:, mh, g, :],
-                )
+        def prepare_w_hid(mh):
+            for piece in range(512 // W_PIECE):
+                c0 = piece * W_PIECE
+                for g in range(PASSES):
+                    regroup(
+                        w_grouped[:, mh, g, c0 * PACK : (c0 + W_PIECE) * PACK].rearrange("p (c t) -> p c t", t=PACK),
+                        w_raw[:, mh, g, :, c0 : c0 + W_PIECE],
+                    )
+                for g in range(PASSES):
+                    nc.vector.quantize_mx(
+                        out=w_codes[:, g, 512 * mh + c0 : 512 * mh + c0 + W_PIECE].bitcast(FP8X4),
+                        scales=w_scales[:, g, 512 * mh + c0 : 512 * mh + c0 + W_PIECE],
+                        in_=w_grouped[:, mh, g, c0 * PACK : (c0 + W_PIECE) * PACK],
+                    )
 
         def hidden_matmuls(mh, bh):
             cols = slice(bh * B_HALF, (bh + 1) * B_HALF)
@@ -170,13 +173,17 @@ def tile_additivecoupling_pa_kernel(tc, x, h_prev, w_hid, b_hid, w_out, b_out, o
                     out=h_rows[:, mh, t, cols], in_=acc[:], func=RELU, bias=bias_col[:, mt : mt + 1], scale=1.0
                 )
 
-        def quantise_hidden(mh, bh):
+        def regroup_hidden(mh, bh):
             cols = slice(bh * B_HALF, (bh + 1) * B_HALF)
             wide = slice(bh * B_HALF * PACK, (bh + 1) * B_HALF * PACK)
             regroup(
                 h_grouped[:, mh, wide].rearrange("p (c t) -> p c t", t=PACK),
                 h_rows[:, mh, :, cols],
             )
+
+        def quantise_hidden(mh, bh):
+            cols = slice(bh * B_HALF, (bh + 1) * B_HALF)
+            wide = slice(bh * B_HALF * PACK, (bh + 1) * B_HALF * PACK)
             nc.vector.quantize_mx(
                 out=h_codes[:, mh, cols].bitcast(FP8X4), scales=h_scales[:, mh, cols], in_=h_grouped[:, mh, wide]
             )
@@ -228,26 +235,32 @@ def tile_additivecoupling_pa_kernel(tc, x, h_prev, w_hid, b_hid, w_out, b_out, o
                     scale=1.0,
                 )
 
-        def couple(bt):
-            rows = slice(bt * P, (bt + 1) * P)
-            bank = y_banks[bt % 2]
-            for jt in range(J_TILES):
-                nc.tensor.transpose(bank[:, 1 + jt, :], shift_t[:, jt, rows], ident_f32[:])
-            y = y_pool.tile([P, D], F32)
-            for jt in range(J_TILES):
+        def couple(bh, jt):
+            step = bh * J_TILES + jt
+            cols = slice(2 * P * jt, 2 * P * (jt + 1))
+            for pair in range(2):
+                bank = y_banks[2 * (step % 2) + pair]
+                for k in range(2):
+                    bt = 4 * bh + 2 * pair + k
+                    nc.tensor.transpose(bank[:, 2 * k + 1, :], shift_t[:, jt, bt * P : (bt + 1) * P], ident_f32[:])
+            for pair in range(2):
+                bank = y_banks[2 * (step % 2) + pair]
+                bt = 4 * bh + 2 * pair
+                y = y_pool.tile([P, 2, 2 * P], F32)
                 nc.vector.tensor_tensor(
-                    out=y[:, 2 * P * jt : 2 * P * (jt + 1)].rearrange("p (j e) -> p j e", e=2),
-                    in0=bank[:, 0 : 2 + jt : 1 + jt, :].rearrange("p e j -> p j e"),
-                    in1=x_rows[:, bt, 2 * P * jt : 2 * P * (jt + 1)].rearrange("p (j e) -> p j e", e=2),
+                    out=y[:].rearrange("p k (j e) -> p k j e", e=2),
+                    in0=bank[:].rearrange("p (k e) j -> p k j e", e=2),
+                    in1=x_rows[:, bt : bt + 2, cols].rearrange("p k (j e) -> p k j e", e=2),
                     op=ADD,
                 )
-            nc.sync.dma_start(out=out[rows, :], in_=y[:])
+                nc.sync.dma_start(
+                    out=out[bt * P : (bt + 2) * P, cols].rearrange("(k p) c -> p k c", p=P), in_=y[:]
+                )
 
         with tc.manual_schedule():
-            regroup_w_hid(0)
+            prepare_w_hid(0)
             transpose_h_prev(0)
             transpose_h_prev(1)
-            quantise_w_hid(0)
             quantise_h_prev(0)
             transpose_h_prev(2)
             transpose_h_prev(3)
@@ -257,23 +270,27 @@ def tile_additivecoupling_pa_kernel(tc, x, h_prev, w_hid, b_hid, w_out, b_out, o
             for bt in range(4, 8):
                 transpose_h_prev(bt)
             hidden_matmuls(0, 0)
-            quantise_w_out()
             quantise_h_prev(2)
+            quantise_w_out()
             quantise_h_prev(3)
-            regroup_w_hid(1)
-            quantise_w_hid(1)
+            prepare_w_hid(1)
             hidden_matmuls(0, 1)
-            quantise_hidden(0, 0)
+            regroup_hidden(0, 0)
             hidden_matmuls(1, 0)
-            quantise_hidden(0, 1)
+            regroup_hidden(0, 1)
+            quantise_hidden(0, 0)
             hidden_matmuls(1, 1)
+            regroup_hidden(1, 0)
             quantise_hidden(1, 0)
             shift_0 = open_shift(0)
             close_shift(shift_0, 0)
-            shift_1 = open_shift(1)
+            quantise_hidden(0, 1)
+            regroup_hidden(1, 1)
             quantise_hidden(1, 1)
-            couple(0)
-            couple(1)
+            couple(0, 0)
+            shift_1 = open_shift(1)
+            couple(0, 1)
             close_shift(shift_1, 1)
-            for bt in range(2, 8):
-                couple(bt)
+            couple(0, 2)
+            for jt in range(J_TILES):
+                couple(1, jt)

@@ -74,8 +74,11 @@ def tile_additivecoupling_pa_kernel(tc, x, h_prev, w_hid, b_hid, w_out, b_out, o
             out=bias_rows[MID_TILES : MID_TILES + J_TILES, :], in_=b_out.rearrange("(m p) -> m p", p=P)
         )
 
-        def load_h_prev(bt):
-            nc.sync.dma_start(out=hp_rows[:, bt, :], in_=h_prev[bt * P : (bt + 1) * P, :])
+        def load_h_prev(duo):
+            nc.sync.dma_start(
+                out=hp_rows[:, 2 * duo : 2 * duo + 2, :],
+                in_=h_prev[2 * P * duo : 2 * P * (duo + 1), :].rearrange("(p k) c -> p k c", k=2),
+            )
 
         def load_w_hid(mh):
             for g in range(PASSES):
@@ -87,19 +90,19 @@ def tile_additivecoupling_pa_kernel(tc, x, h_prev, w_hid, b_hid, w_out, b_out, o
                     )
 
         load_w_hid(0)
-        for bt in range(4):
-            load_h_prev(bt)
+        for duo in range(2):
+            load_h_prev(duo)
         nc.sync.dma_start(
             out=wo_raw[:].rearrange("p g t n -> p (g t) n"),
             in_=w_out.rearrange("(s p) n -> p s n", p=P),
         )
-        for bt in range(4, 8):
-            load_h_prev(bt)
+        for duo in range(2, 4):
+            load_h_prev(duo)
         load_w_hid(1)
         for xh in range(2):
             nc.sync.dma_start(
-                out=x_rows[:, 4 * xh : 4 * xh + 4, :],
-                in_=x[B_HALF * xh : B_HALF * (xh + 1), :].rearrange("(t p) d -> p t d", p=P),
+                out=x_rows[:, 4 * xh : 4 * xh + 4, :].rearrange("p (c k) d -> p c (k d)", k=2),
+                in_=x[B_HALF * xh : B_HALF * (xh + 1), :].rearrange("(c p k) d -> p c (k d)", p=P, k=2),
             )
 
         make_identity(nc, ident_f32[:])
@@ -254,7 +257,7 @@ def tile_additivecoupling_pa_kernel(tc, x, h_prev, w_hid, b_hid, w_out, b_out, o
                     op=ADD,
                 )
                 nc.sync.dma_start(
-                    out=out[bt * P : (bt + 2) * P, cols].rearrange("(k p) c -> p k c", p=P), in_=y[:]
+                    out=out[bt * P : (bt + 2) * P, cols].rearrange("(p k) c -> p k c", k=2), in_=y[:]
                 )
 
         with tc.manual_schedule():

from contextlib import ExitStack

import concourse.mybir as mybir
from concourse.masks import make_identity

F32 = mybir.dt.float32
BF16 = mybir.dt.bfloat16
U32 = mybir.dt.uint32
U8 = mybir.dt.uint8
FP8X4 = mybir.dt.float8_e4m3fn_x4
ADD = mybir.AluOpType.add
RELU = mybir.ActivationFunctionType.Relu
IDENTITY = mybir.ActivationFunctionType.Identity

P = 128
PACK = 4
K_PASS = P * PACK
B, D, MP, MID = 1024, 768, 1024, 1024
HALF = D // 2
B_TILES = B // P
B_HALF = 512
PASSES = MP // K_PASS
MID_TILES = MID // P
J_TILES = HALF // P
Y_BANKS = 4
W_PIECE = 256

FLOPS = 2 * B * MP * MID + 2 * B * MID * HALF


def tile_additivecoupling_pa_kernel(tc, x, h_prev, w_hid, b_hid, w_out, b_out, out):
    nc = tc.nc
    with ExitStack() as ctx:
        keep = ctx.enter_context(tc.tile_pool(name="keep", bufs=1))
        y_pool = ctx.enter_context(tc.tile_pool(name="y_pool", bufs=12))
        psum_acc = ctx.enter_context(tc.psum_pool(name="psum_acc", bufs=4))
        psum_y = ctx.enter_context(tc.psum_pool(name="psum_y", bufs=1))

        hp_rows = keep.tile([P, B_TILES, MP], BF16)
        hp_grouped = keep.tile([P, PASSES, B * PACK], BF16, align_bytes=64)
        hp_codes = keep.tile([P, PASSES, B], U32, align_bytes=64)
        hp_scales = keep.tile([P, PASSES, B], U8, align_bytes=64)

        w_raw = keep.tile([P, 2, PASSES, PACK, 512], BF16)
        w_grouped = keep.tile([P, 2, PASSES, 512 * PACK], BF16, align_bytes=64)
        w_codes = keep.tile([P, PASSES, MID], U32, align_bytes=64)
        w_scales = keep.tile([P, PASSES, MID], U8, align_bytes=64)

        h_rows = keep.tile([P, PASSES, PACK, B], BF16)
        h_grouped = keep.tile([P, PASSES, B * PACK], BF16, align_bytes=64)
        h_codes = keep.tile([P, PASSES, B], U32, align_bytes=64)
        h_scales = keep.tile([P, PASSES, B], U8, align_bytes=64)

        wo_raw = keep.tile([P, PASSES, PACK, HALF], BF16)
        wo_grouped = keep.tile([P, PASSES * HALF * PACK], BF16, align_bytes=64)
        wo_codes = keep.tile([P, PASSES * HALF], U32, align_bytes=64)
        wo_scales = keep.tile([P, PASSES * HALF], U8, align_bytes=64)

        x_rows = keep.tile([P, B_TILES, D], BF16)
        shift_t = keep.tile([P, J_TILES, B], F32)

        ident_f32 = keep.tile([P, P], F32)
        ident_bf16 = keep.tile([P, P], BF16)
        zeros_f32 = keep.tile([P, P], F32)
        bias_rows = keep.tile([P, P], BF16)
        bias_col = keep.tile([P, MID_TILES + J_TILES], F32)

        y_banks = [psum_y.tile([P, 4, P], F32, name="y_bank%d" % i) for i in range(Y_BANKS)]

        nc.vector.memset(bias_rows[:], 0.0)
        nc.vector.memset(zeros_f32[:], 0.0)
        nc.scalar.dma_start(out=bias_rows[0:MID_TILES, :], in_=b_hid.rearrange("(m p) -> m p", p=P))
        nc.scalar.dma_start(
            out=bias_rows[MID_TILES : MID_TILES + J_TILES, :], in_=b_out.rearrange("(m p) -> m p", p=P)
        )

        def load_h_prev(duo):
            nc.sync.dma_start(
                out=hp_rows[:, 2 * duo : 2 * duo + 2, :],
                in_=h_prev[2 * P * duo : 2 * P * (duo + 1), :].rearrange("(p k) c -> p k c", k=2),
            )

        def load_w_hid(mh):
            for g in range(PASSES):
                for u in range(2):
                    r0 = K_PASS * g + 256 * u
                    nc.sync.dma_start(
                        out=w_raw[:, mh, g, 2 * u : 2 * u + 2, :],
                        in_=w_hid[r0 : r0 + 256, 512 * mh : 512 * mh + 512].rearrange("(q e) c -> q e c", e=2),
                    )

        load_w_hid(0)
        for duo in range(2):
            load_h_prev(duo)
        nc.sync.dma_start(
            out=wo_raw[:].rearrange("p g t n -> p (g t) n"),
            in_=w_out.rearrange("(s p) n -> p s n", p=P),
        )
        for duo in range(2, 4):
            load_h_prev(duo)
        load_w_hid(1)
        for xh in range(2):
            nc.sync.dma_start(
                out=x_rows[:, 4 * xh : 4 * xh + 4, :].rearrange("p (c k) d -> p c (k d)", k=2),
                in_=x[B_HALF * xh : B_HALF * (xh + 1), :].rearrange("(c p k) d -> p c (k d)", p=P, k=2),
            )

        make_identity(nc, ident_f32[:])
        nc.vector.tensor_copy(out=ident_bf16[:], in_=ident_f32[:])

        def spread_biases():
            bias_t = psum_acc.tile([P, P], BF16, tag="acc")
            nc.tensor.transpose(bias_t[:], bias_rows[:], ident_bf16[:])
            nc.vector.tensor_copy(out=bias_col[:], in_=bias_t[:, 0 : MID_TILES + J_TILES])
            for bank in y_banks:
                for k in range(2):
                    nc.tensor.transpose(bank[:, 2 * k, :], zeros_f32[:], ident_f32[:])

        def transpose_h_prev(bt):
            words = hp_rows[:, bt, :].bitcast(F32)
            pairs_t = psum_acc.tile([P, 2 * PASSES, P], F32, tag="acc")
            for s in range(2 * PASSES):
                nc.tensor.transpose(pairs_t[:, s, :], words[:, s * P : (s + 1) * P], ident_f32[:])
            nc.scalar.copy(
                out=hp_grouped[:, :, bt * P * PACK : (bt + 1) * P * PACK]
                .bitcast(F32)
                .rearrange("q g (b u) -> q g b u", u=2),
                in_=pairs_t[:].rearrange("q (g u) b -> q g b u", u=2),
            )

        def quantise_h_prev(pair):
            cols = slice(pair * 2 * P, (pair + 1) * 2 * P)
            wide = slice(pair * 2 * P * PACK, (pair + 1) * 2 * P * PACK)
            for g in range(PASSES):
                nc.vector.quantize_mx(
                    out=hp_codes[:, g, cols].bitcast(FP8X4), scales=hp_scales[:, g, cols], in_=hp_grouped[:, g, wide]
                )

        def regroup(dst, src):
            nc.vector.tensor_copy(
                out=dst.rearrange("p (c i) t -> p c t i", i=4),
                in_=src.rearrange("p t (c i) -> p c t i", i=4),
            )

        def prepare_w_hid(mh):
            for piece in range(512 // W_PIECE):
                c0 = piece * W_PIECE
                for g in range(PASSES):
                    regroup(
                        w_grouped[:, mh, g, c0 * PACK : (c0 + W_PIECE) * PACK].rearrange("p (c t) -> p c t", t=PACK),
                        w_raw[:, mh, g, :, c0 : c0 + W_PIECE],
                    )
                for g in range(PASSES):
                    nc.vector.quantize_mx(
                        out=w_codes[:, g, 512 * mh + c0 : 512 * mh + c0 + W_PIECE].bitcast(FP8X4),
                        scales=w_scales[:, g, 512 * mh + c0 : 512 * mh + c0 + W_PIECE],
                        in_=w_grouped[:, mh, g, c0 * PACK : (c0 + W_PIECE) * PACK],
                    )

        def hidden_matmuls(mh, bh):
            cols = slice(bh * B_HALF, (bh + 1) * B_HALF)
            for t in range(PACK):
                mt = PACK * mh + t
                acc = psum_acc.tile([P, B_HALF], F32, tag="acc")
                for g in range(PASSES):
                    nc.tensor.matmul_mx(
                        out=acc[:],
                        lhsT=w_codes[:, g, mt * P : (mt + 1) * P].bitcast(FP8X4),
                        lhsT_scale=w_scales[:, g, mt * P : (mt + 1) * P],
                        rhs=hp_codes[:, g, cols].bitcast(FP8X4),
                        rhs_scale=hp_scales[:, g, cols],
                        start=(g == 0),
                        stop=(g == PASSES - 1),
                    )
                nc.scalar.activation(
                    out=h_rows[:, mh, t, cols], in_=acc[:], func=RELU, bias=bias_col[:, mt : mt + 1], scale=1.0
                )

        def regroup_hidden(mh, bh):
            cols = slice(bh * B_HALF, (bh + 1) * B_HALF)
            wide = slice(bh * B_HALF * PACK, (bh + 1) * B_HALF * PACK)
            regroup(
                h_grouped[:, mh, wide].rearrange("p (c t) -> p c t", t=PACK),
                h_rows[:, mh, :, cols],
            )

        def quantise_hidden(mh, bh):
            cols = slice(bh * B_HALF, (bh + 1) * B_HALF)
            wide = slice(bh * B_HALF * PACK, (bh + 1) * B_HALF * PACK)
            nc.vector.quantize_mx(
                out=h_codes[:, mh, cols].bitcast(FP8X4), scales=h_scales[:, mh, cols], in_=h_grouped[:, mh, wide]
            )

        def regroup_w_out():
            for g in range(PASSES):
                regroup(
                    wo_grouped[:, g * HALF * PACK : (g + 1) * HALF * PACK].rearrange("p (c t) -> p c t", t=PACK),
                    wo_raw[:, g, :, :],
                )

        def quantise_w_out():
            for c0, c1 in ((0, 512), (512, PASSES * HALF)):
                nc.vector.quantize_mx(
                    out=wo_codes[:, c0:c1].bitcast(FP8X4),
                    scales=wo_scales[:, c0:c1],
                    in_=wo_grouped[:, c0 * PACK : c1 * PACK],
                )

        def shift_pass(acc, jt, bh, g):
            cols = slice(bh * B_HALF, (bh + 1) * B_HALF)
            w0 = g * HALF + jt * P
            nc.tensor.matmul_mx(
                out=acc[:],
                lhsT=wo_codes[:, w0 : w0 + P].bitcast(FP8X4),
                lhsT_scale=wo_scales[:, w0 : w0 + P],
                rhs=h_codes[:, g, cols].bitcast(FP8X4),
                rhs_scale=h_scales[:, g, cols],
                start=(g == 0),
                stop=(g == PASSES - 1),
            )

        def open_shift(bh):
            accs = [psum_acc.tile([P, B_HALF], F32, tag="acc", name="shift_acc%d" % jt) for jt in range(J_TILES)]
            for jt in range(J_TILES):
                shift_pass(accs[jt], jt, bh, 0)
            return accs

        def close_shift(accs, bh):
            cols = slice(bh * B_HALF, (bh + 1) * B_HALF)
            for jt in range(J_TILES):
                acc = accs[jt]
                shift_pass(acc, jt, bh, 1)
                nc.scalar.activation(
                    out=shift_t[:, jt, cols],
                    in_=acc[:],
                    func=IDENTITY,
                    bias=bias_col[:, MID_TILES + jt : MID_TILES + jt + 1],
                    scale=1.0,
                )

        def couple(bh, jt):
            step = bh * J_TILES + jt
            cols = slice(2 * P * jt, 2 * P * (jt + 1))
            for pair in range(2):
                bank = y_banks[2 * (step % 2) + pair]
                for k in range(2):
                    bt = 4 * bh + 2 * pair + k
                    nc.tensor.transpose(bank[:, 2 * k + 1, :], shift_t[:, jt, bt * P : (bt + 1) * P], ident_f32[:])
            for pair in range(2):
                bank = y_banks[2 * (step % 2) + pair]
                bt = 4 * bh + 2 * pair
                y = y_pool.tile([P, 2, 2 * P], F32)
                nc.vector.tensor_tensor(
                    out=y[:].rearrange("p k (j e) -> p k j e", e=2),
                    in0=bank[:].rearrange("p (k e) j -> p k j e", e=2),
                    in1=x_rows[:, bt : bt + 2, cols].rearrange("p k (j e) -> p k j e", e=2),
                    op=ADD,
                )
                nc.sync.dma_start(
                    out=out[bt * P : (bt + 2) * P, cols].rearrange("(p k) c -> p k c", k=2), in_=y[:]
                )

        with tc.manual_schedule():
            prepare_w_hid(0)
            transpose_h_prev(0)
            transpose_h_prev(1)
            quantise_h_prev(0)
            transpose_h_prev(2)
            transpose_h_prev(3)
            spread_biases()
            quantise_h_prev(1)
            regroup_w_out()
            for bt in range(4, 8):
                transpose_h_prev(bt)
            hidden_matmuls(0, 0)
            quantise_h_prev(2)
            quantise_w_out()
            quantise_h_prev(3)
            prepare_w_hid(1)
            hidden_matmuls(0, 1)
            regroup_hidden(0, 0)
            hidden_matmuls(1, 0)
            regroup_hidden(0, 1)
            quantise_hidden(0, 0)
            hidden_matmuls(1, 1)
            regroup_hidden(1, 0)
            quantise_hidden(1, 0)
            shift_0 = open_shift(0)
            close_shift(shift_0, 0)
            quantise_hidden(0, 1)
            regroup_hidden(1, 1)
            quantise_hidden(1, 1)
            couple(0, 0)
            shift_1 = open_shift(1)
            couple(0, 1)
            close_shift(shift_1, 1)
            couple(0, 2)
            for jt in range(J_TILES):
                couple(1, jt)
